import numpy as np
import ml_dtypes


def mxq(x, axis, fmt="e4m3"):
    dtype, down = {"e4m3": (ml_dtypes.float8_e4m3fn, 7), "e5m2": (ml_dtypes.float8_e5m2, 14)}[fmt]
    v = np.moveaxis(np.asarray(x, np.float32).astype(ml_dtypes.bfloat16).astype(np.float64), axis, -1)
    blocks = v.reshape(v.shape[:-1] + (-1, 32))
    amax = np.abs(blocks).max(-1, keepdims=True)
    byte = np.maximum(np.where(amax > 0, np.frexp(amax)[1] - 1 + 127, 0) - down, 1)
    scale = np.exp2(byte - 127.0)
    codes = (blocks / scale).astype(np.float32).astype(dtype).astype(np.float64)
    return np.moveaxis((codes * scale).reshape(v.shape), -1, axis)


WIDE = False


def mx_kscale(k):
    if not WIDE:
        return np.ones(k)
    levels = np.array([30, -30])
    if k % 512:
        return np.exp2(np.random.permutation(np.resize(levels, k // 32))).repeat(32)
    a = np.empty((k // 512, 16))
    for p in range(k // 512):
        a[p, :8] = np.random.permutation(np.resize(levels, 8))
        for g in range(8):
            far = levels[np.abs(levels - a[p, g]) >= 10]
            a[p, g + 8] = far[np.random.randint(len(far))]
    return np.exp2(a.ravel()).repeat(32)


BF16 = ml_dtypes.bfloat16


def bf(x):
    return np.asarray(x, np.float32).astype(BF16)


def f64(x):
    return np.asarray(x).astype(np.float64)


S, D, H, DH = 512, 2048, 16, 128
ROPE_BASE = 10000.0


def rotate_half(v):
    shp = v.shape
    p = v.reshape(*shp[:-1], shp[-1] // 2, 2)
    return np.stack((-p[..., 1], p[..., 0]), axis=-1).reshape(shp)


def rope_cos_sin(seq_len, dh):
    inv_freq = 1.0 / (ROPE_BASE ** (np.arange(0, dh, 2) / dh))
    t = np.arange(seq_len)
    freqs = t[:, None] * inv_freq[None, :]
    return np.repeat(np.cos(freqs), 2, axis=-1), np.repeat(np.sin(freqs), 2, axis=-1)


def setup_inputs():
    s = mx_kscale(D)
    return {"x": bf(np.random.standard_normal((S, D)) * s),
            "w": bf(np.random.standard_normal((H * DH, D)) / np.sqrt(D) / s[None, :])}


def reference(x, w):
    y = mxq(f64(x), 1, "e5m2") @ mxq(f64(w), 1, "e4m3").T
    q = y.reshape(S, H, DH).transpose(1, 0, 2)
    cos, sin = rope_cos_sin(S, DH)
    return q * cos[None] + rotate_half(q) * sin[None]

@@ -1,0 +1,238 @@
+from contextlib import ExitStack
+import math
+
+import concourse.mybir as mybir
+from concourse.masks import make_identity
+
+F32 = mybir.dt.float32
+BF16 = mybir.dt.bfloat16
+U32 = mybir.dt.uint32
+U8 = mybir.dt.uint8
+I32 = mybir.dt.int32
+E5X4 = mybir.dt.float8_e5m2_x4
+E4X4 = mybir.dt.float8_e4m3fn_x4
+ALU = mybir.AluOpType
+ACT = mybir.ActivationFunctionType
+
+S_TOK, D_IN, HEADS, DH = 512, 2048, 16, 128
+FLOPS = 2 * S_TOK * D_IN * HEADS * DH
+P = 128
+NJ = 4
+NG = 4
+NGRP = 4
+TWO_PI = 2.0 * math.pi
+C1 = 6.28125
+C2C = 0.0019353628158569336
+C3 = TWO_PI - C1 - C2C
+ADD_ON_GPSIMD = True
+
+
+def tile_attention_pa_kernel(tc, x, w, out):
+    nc = tc.nc
+    with ExitStack() as ctx:
+        const = ctx.enter_context(tc.tile_pool(name="const", bufs=1))
+        raw = ctx.enter_context(tc.tile_pool(name="raw", bufs=1))
+        keep = ctx.enter_context(tc.tile_pool(name="keep", bufs=1))
+        wpool = ctx.enter_context(tc.tile_pool(name="wpool", bufs=2))
+        ep = ctx.enter_context(tc.tile_pool(name="ep", bufs=3))
+        ps_t = ctx.enter_context(tc.psum_pool(name="ps_t", bufs=4))
+        ps_a = ctx.enter_context(tc.psum_pool(name="ps_a", bufs=4))
+        ctx.enter_context(tc.manual_schedule())
+
+        x_v = x.rearrange("(r j) k -> r j k", j=NJ)
+        xr = []
+        wr = []
+        for j in range(NJ):
+            xr.append(raw.tile([P, D_IN], BF16, name="xr%d" % j))
+        for m in range(HEADS):
+            wr.append(raw.tile([P, D_IN], BF16, name="wr%d" % m))
+
+        def load_x(j):
+            nc.sync.dma_start(out=xr[j][:], in_=x_v[:, j, :])
+
+        def load_w(m):
+            nc.sync.dma_start(out=wr[m][:], in_=w[P * m:P * (m + 1), :])
+
+        load_x(0)
+        load_x(1)
+        for m in range(4):
+            load_w(m)
+        load_x(2)
+        load_x(3)
+        for m in range(4, HEADS):
+            load_w(m)
+
+        ident = const.tile([P, P], F32, name="ident")
+        make_identity(nc, ident[:])
+        idx_i = const.tile([P, NJ], I32, name="idx_i")
+        nc.gpsimd.iota(idx_i[:], pattern=[[1, NJ]], base=0, channel_multiplier=NJ)
+
+        dm = const.tile([P, 2], F32, name="dm")
+        nc.vector.memset(dm[:], 0.0)
+        nc.scalar.activation(out=dm[:, 1:2], in_=dm[:, 0:1], func=ACT.Sin)
+
+        idx_f = const.tile([P, NJ], F32, name="idx_f")
+        nc.vector.tensor_copy(out=idx_f[:], in_=idx_i[:])
+        th = const.tile([P, 64], F32, name="th")
+        nc.vector.memset(th[:, 0:1], 1.0)
+        q = 10000.0 ** (-1.0 / 64.0)
+        for s in range(6):
+            wd = 1 << s
+            nc.vector.tensor_scalar(out=th[:, wd:2 * wd], in0=th[:, 0:wd], scalar1=q ** wd,
+                                    scalar2=None, op0=ALU.mult)
+        ang = const.tile([P, NJ, 64], F32, name="ang")
+        for j in range(NJ):
+            nc.vector.tensor_scalar(out=ang[:, j, :], in0=th[:], scalar1=idx_f[:, j:j + 1],
+                                    scalar2=None, op0=ALU.mult)
+        n_i = const.tile([P, NJ, 64], I32, name="n_i")
+        nc.vector.tensor_scalar(out=n_i[:], in0=ang[:], scalar1=1.0 / TWO_PI, scalar2=None,
+                                op0=ALU.mult)
+        n_f = const.tile([P, NJ, 64], F32, name="n_f")
+        nc.vector.tensor_copy(out=n_f[:], in_=n_i[:])
+        r1 = const.tile([P, NJ, 64], F32, name="r1")
+        nc.vector.scalar_tensor_tensor(out=r1[:], in0=n_f[:], scalar=-C1, in1=ang[:],
+                                       op0=ALU.mult, op1=ALU.add)
+        r2 = const.tile([P, NJ, 64], F32, name="r2")
+        nc.vector.scalar_tensor_tensor(out=r2[:], in0=n_f[:], scalar=-C2C, in1=r1[:],
+                                       op0=ALU.mult, op1=ALU.add)
+        r3 = const.tile([P, NJ, 64], F32, name="r3")
+        nc.vector.scalar_tensor_tensor(out=r3[:], in0=n_f[:], scalar=-C3, in1=r2[:],
+                                       op0=ALU.mult, op1=ALU.add)
+        fd = const.tile([P, NJ, 64], F32, name="fd")
+        nc.vector.tensor_scalar(out=fd[:], in0=r3[:], scalar1=math.pi, scalar2=-TWO_PI,
+                                op0=ALU.is_gt, op1=ALU.mult)
+        r4 = const.tile([P, NJ, 64], F32, name="r4")
+        nc.vector.tensor_tensor(out=r4[:], in0=r3[:], in1=fd[:], op=ALU.add)
+        ab = const.tile([P, NJ, 64], F32, name="ab")
+        nc.vector.scalar_tensor_tensor(out=ab[:], in0=r4[:], scalar=-1.0, in1=r4[:],
+                                       op0=ALU.mult, op1=ALU.max)
+        sin_t = const.tile([P, NJ, 64], F32, name="sin_t")
+        cos_t = const.tile([P, NJ, 64], F32, name="cos_t")
+        cos2 = const.tile([P, NJ, 64, 2], F32, name="cos2")
+        sin2 = const.tile([P, NJ, 64, 2], F32, name="sin2")
+
+        def table_scalar():
+            nc.scalar.activation(out=sin_t[:], in_=r4[:], func=ACT.Sin)
+            nc.scalar.activation(out=cos_t[:], in_=ab[:], func=ACT.Sin, bias=math.pi / 2.0,
+                                 scale=-1.0)
+
+        def table_expand():
+            nc.vector.tensor_copy(out=cos2[:, :, :, 0], in_=cos_t[:])
+            nc.vector.tensor_copy(out=cos2[:, :, :, 1], in_=cos_t[:])
+            nc.vector.tensor_scalar(out=sin2[:, :, :, 0], in0=sin_t[:], scalar1=-1.0,
+                                    scalar2=None, op0=ALU.mult)
+            nc.vector.tensor_copy(out=sin2[:, :, :, 1], in_=sin_t[:])
+
+        xg = keep.tile([P, NJ, NG, P, 2], F32, name="xg", align_bytes=64)
+        xc = keep.tile([P, NJ, NG, P], U32, name="xc", align_bytes=64)
+        xs = keep.tile([P, NJ, NG, P], U8, name="xs", align_bytes=64)
+
+        def copy_out(eng, dst, src):
+            if eng == "s":
+                nc.scalar.copy(out=dst, in_=src)
+            else:
+                nc.vector.tensor_copy(out=dst, in_=src)
+
+        def t_x(j, engs):
+            words = xr[j][:].bitcast(F32)
+            for gp in range(2):
+                bank = ps_t.tile([P, 2, 2, P], F32, name="tbank")
+                for gg in range(2):
+                    g = 2 * gp + gg
+                    for u in range(2):
+                        nc.tensor.transpose(bank[:, gg, u, :],
+                                            words[:, 256 * g + u:256 * (g + 1):2], ident[:])
+                copy_out(engs[gp], xg[:, j, 2 * gp:2 * gp + 2, :, :],
+                         bank.rearrange("p g u r -> p g r u"))
+
+        def q_x(j):
+            nc.vector.quantize_mx(
+                out=xc[:, j].rearrange("p g r -> p (g r)").bitcast(E5X4),
+                scales=xs[:, j].rearrange("p g r -> p (g r)"),
+                in_=xg[:, j].rearrange("p g r u -> p (g r u)").bitcast(BF16))
+
+        wg = {}
+        wc = {}
+        ws = {}
+
+        def t_w(n, hlf, engs):
+            if hlf == 0:
+                wg[n] = wpool.tile([P, NG, 512, 2], F32, name="wg", align_bytes=64)
+                wc[n] = wpool.tile([P, NG, 512], U32, name="wc", align_bytes=64)
+                ws[n] = wpool.tile([P, NG, 512], U8, name="ws", align_bytes=64)
+            for g in range(NG):
+                bank = ps_t.tile([P, 2, 2, P], F32, name="tbank")
+                for mm in range(2):
+                    words = wr[4 * n + 2 * hlf + mm][:].bitcast(F32)
+                    for u in range(2):
+                        nc.tensor.transpose(bank[:, mm, u, :],
+                                            words[:, 256 * g + u:256 * (g + 1):2], ident[:])
+                dst = wg[n][:, g, 256 * hlf:256 * (hlf + 1), :]
+                copy_out(engs[g], dst.rearrange("p (m d) u -> p m d u", m=2),
+                         bank.rearrange("p m u d -> p m d u"))
+
+        def q_w(n, hlf):
+            cols = slice(256 * hlf, 256 * (hlf + 1))
+            for g in range(NG):
+                nc.vector.quantize_mx(
+                    out=wc[n][:, g, cols].bitcast(E4X4),
+                    scales=ws[n][:, g, cols],
+                    in_=wg[n][:, g, cols, :].rearrange("p f u -> p (f u)").bitcast(BF16))
+
+        acc = {}
+        out_v = out.rearrange("h (r j) d -> r h j d", j=NJ)
+
+        def mm(n, jp):
+            for jj in range(2):
+                j = 2 * jp + jj
+                a = ps_a.tile([P, 512], F32, name="acc")
+                acc[(n, j)] = a
+                for g in range(NG):
+                    nc.tensor.matmul_mx(out=a[:], lhsT=xc[:, j, g, :].bitcast(E5X4),
+                                        lhsT_scale=xs[:, j, g, :],
+                                        rhs=wc[n][:, g, :].bitcast(E4X4),
+                                        rhs_scale=ws[n][:, g, :],
+                                        start=(g == 0), stop=(g == NG - 1))
+
+        def rope(n, jp):
+            res = ep.tile([P, 4, 2, DH], F32, name="res")
+            for jj in range(2):
+                j = 2 * jp + jj
+                a4 = acc[(n, j)].rearrange("p (h n e) -> p h n e", h=4, e=2)
+                t1 = ep.tile([P, 4, 64, 2], F32, name="t1")
+                t2 = ep.tile([P, 4, 64, 2], F32, name="t2")
+                nc.vector.tensor_tensor(out=t1[:], in0=a4,
+                                        in1=cos2[:, j].unsqueeze(1).to_broadcast([P, 4, 64, 2]),
+                                        op=ALU.mult)
+                nc.vector.tensor_tensor(out=t2[:], in0=a4[:, :, :, ::-1],
+                                        in1=sin2[:, j].unsqueeze(1).to_broadcast([P, 4, 64, 2]),
+                                        op=ALU.mult)
+                add_eng = nc.gpsimd if ADD_ON_GPSIMD else nc.vector
+                add_eng.tensor_tensor(out=res[:, :, jj, :],
+                                      in0=t1.rearrange("p h n e -> p h (n e)"),
+                                      in1=t2.rearrange("p h n e -> p h (n e)"), op=ALU.add)
+            nc.sync.dma_start(out=out_v[:, 4 * n:4 * n + 4, 2 * jp:2 * jp + 2, :], in_=res[:])
+
+        t_x(0, "ss")
+        t_x(1, "ss")
+        table_scalar()
+        q_x(0)
+        q_x(1)
+        table_expand()
+        t_w(0, 0, "sssv")
+        q_w(0, 0)
+        t_w(0, 1, "sssv")
+        q_w(0, 1)
+        t_x(2, "ss")
+        t_x(3, "sv")
+        q_x(2)
+        q_x(3)
+        t_w(1, 0, "sssv")
+        q_w(1, 0)
+        t_list = [(1, 1), (2, 0), (2, 1), (3, 0), (3, 1)]
+        for k in range(8):
+            mm(k // 2, k % 2)
+            rope(k // 2, k % 2)
+            if k < len(t_list):
+                t_w(t_list[k][0], t_list[k][1], "ssss")
+                q_w(t_list[k][0], t_list[k][1])

@@ -24,7 +24,6 @@ TWO_PI = 2.0 * math.pi
 C1 = 6.28125
 C2C = 0.0019353628158569336
 C3 = TWO_PI - C1 - C2C
-ADD_ON_GPSIMD = True
 
 
 def tile_attention_pa_kernel(tc, x, w, out):
@@ -43,12 +42,13 @@ def tile_attention_pa_kernel(tc, x, w, out):
         xr = []
         wr = []
         for j in range(NJ):
-            xr.append(raw.tile([P, D_IN], BF16, name="xr%d" % j))
+            xr.append([raw.tile([P, D_IN // 2], BF16, name="xr%d_%d" % (j, c)) for c in range(2)])
         for m in range(HEADS):
             wr.append(raw.tile([P, D_IN], BF16, name="wr%d" % m))
 
         def load_x(j):
-            nc.sync.dma_start(out=xr[j][:], in_=x_v[:, j, :])
+            for c in range(2):
+                nc.sync.dma_start(out=xr[j][c][:], in_=x_v[:, j, 1024 * c:1024 * (c + 1)])
 
         def load_w(m):
             nc.sync.dma_start(out=wr[m][:], in_=w[P * m:P * (m + 1), :])
@@ -61,6 +61,16 @@ def tile_attention_pa_kernel(tc, x, w, out):
         load_x(3)
         for m in range(4, HEADS):
             load_w(m)
+
+        dz = const.tile([P, 512], BF16, name="dz")
+        nc.vector.memset(dz[:], 0.0)
+        dacc = ps_a.tile([P, 512], F32, name="acc")
+
+        def dummy(count):
+            for i in range(count):
+                nc.tensor.matmul(out=dacc[:], lhsT=dz[:, 0:P], rhs=dz[:], start=True, stop=True)
+
+        dummy(6)
 
         ident = const.tile([P, P], F32, name="ident")
         make_identity(nc, ident[:])
@@ -134,14 +144,13 @@ def tile_attention_pa_kernel(tc, x, w, out):
                 nc.vector.tensor_copy(out=dst, in_=src)
 
         def t_x(j, engs):
-            words = xr[j][:].bitcast(F32)
             for gp in range(2):
+                words = xr[j][gp][:].bitcast(F32)
                 bank = ps_t.tile([P, 2, 2, P], F32, name="tbank")
                 for gg in range(2):
-                    g = 2 * gp + gg
                     for u in range(2):
                         nc.tensor.transpose(bank[:, gg, u, :],
-                                            words[:, 256 * g + u:256 * (g + 1):2], ident[:])
+                                            words[:, 256 * gg + u:256 * (gg + 1):2], ident[:])
                 copy_out(engs[gp], xg[:, j, 2 * gp:2 * gp + 2, :, :],
                          bank.rearrange("p g u r -> p g r u"))
 
@@ -155,7 +164,7 @@ def tile_attention_pa_kernel(tc, x, w, out):
         wc = {}
         ws = {}
 
-        def t_w(n, hlf, engs):
+        def t_w(n, hlf, engs, warm=0):
             if hlf == 0:
                 wg[n] = wpool.tile([P, NG, 512, 2], F32, name="wg", align_bytes=64)
                 wc[n] = wpool.tile([P, NG, 512], U32, name="wc", align_bytes=64)
@@ -170,6 +179,10 @@ def tile_attention_pa_kernel(tc, x, w, out):
                 dst = wg[n][:, g, 256 * hlf:256 * (hlf + 1), :]
                 copy_out(engs[g], dst.rearrange("p (m d) u -> p m d u", m=2),
                          bank.rearrange("p m u d -> p m d u"))
+                if g == 1 and warm >= 1:
+                    dummy(1)
+                if g == 3 and warm >= 2:
+                    dummy(1)
 
         def q_w(n, hlf):
             cols = slice(256 * hlf, 256 * (hlf + 1))
@@ -194,7 +207,7 @@ def tile_attention_pa_kernel(tc, x, w, out):
                                         rhs_scale=ws[n][:, g, :],
                                         start=(g == 0), stop=(g == NG - 1))
 
-        def rope(n, jp):
+        def rope(n, jp, adders, split_store):
             res = ep.tile([P, 4, 2, DH], F32, name="res")
             for jj in range(2):
                 j = 2 * jp + jj
@@ -207,32 +220,39 @@ def tile_attention_pa_kernel(tc, x, w, out):
                 nc.vector.tensor_tensor(out=t2[:], in0=a4[:, :, :, ::-1],
                                         in1=sin2[:, j].unsqueeze(1).to_broadcast([P, 4, 64, 2]),
                                         op=ALU.mult)
-                add_eng = nc.gpsimd if ADD_ON_GPSIMD else nc.vector
+                add_eng = nc.gpsimd if adders[jj] == "g" else nc.vector
                 add_eng.tensor_tensor(out=res[:, :, jj, :],
                                       in0=t1.rearrange("p h n e -> p h (n e)"),
                                       in1=t2.rearrange("p h n e -> p h (n e)"), op=ALU.add)
-            nc.sync.dma_start(out=out_v[:, 4 * n:4 * n + 4, 2 * jp:2 * jp + 2, :], in_=res[:])
+                if split_store:
+                    nc.sync.dma_start(out=out_v[:, 4 * n:4 * n + 4, j, :], in_=res[:, :, jj, :])
+            if not split_store:
+                nc.sync.dma_start(out=out_v[:, 4 * n:4 * n + 4, 2 * jp:2 * jp + 2, :], in_=res[:])
 
         t_x(0, "ss")
+        dummy(2)
         t_x(1, "ss")
+        dummy(1)
         table_scalar()
         q_x(0)
         q_x(1)
         table_expand()
-        t_w(0, 0, "sssv")
+        t_w(0, 0, "sssv", 2)
         q_w(0, 0)
-        t_w(0, 1, "sssv")
+        t_w(0, 1, "sssv", 2)
         q_w(0, 1)
         t_x(2, "ss")
+        dummy(1)
         t_x(3, "sv")
+        dummy(1)
         q_x(2)
         q_x(3)
-        t_w(1, 0, "sssv")
+        t_w(1, 0, "sssv", 1)
         q_w(1, 0)
         t_list = [(1, 1), (2, 0), (2, 1), (3, 0), (3, 1)]
         for k in range(8):
             mm(k // 2, k % 2)
-            rope(k // 2, k % 2)
+            rope(k // 2, k % 2, "gv" if k == 7 else "gg", k == 7)
             if k < len(t_list):
                 t_w(t_list[k][0], t_list[k][1], "ssss")
                 q_w(t_list[k][0], t_list[k][1])

@@ -34,6 +34,7 @@ def tile_attention_pa_kernel(tc, x, w, out):
         keep = ctx.enter_context(tc.tile_pool(name="keep", bufs=1))
         wpool = ctx.enter_context(tc.tile_pool(name="wpool", bufs=2))
         ep = ctx.enter_context(tc.tile_pool(name="ep", bufs=3))
+        ppool = ctx.enter_context(tc.tile_pool(name="ppool", bufs=4))
         ps_t = ctx.enter_context(tc.psum_pool(name="ps_t", bufs=4))
         ps_a = ctx.enter_context(tc.psum_pool(name="ps_a", bufs=4))
         ctx.enter_context(tc.manual_schedule())
@@ -42,23 +43,25 @@ def tile_attention_pa_kernel(tc, x, w, out):
         xr = []
         wr = []
         for j in range(NJ):
-            xr.append([raw.tile([P, D_IN // 2], BF16, name="xr%d_%d" % (j, c)) for c in range(2)])
+            xr.append(raw.tile([P, D_IN], BF16, name="xr%d" % j))
         for m in range(HEADS):
             wr.append(raw.tile([P, D_IN], BF16, name="wr%d" % m))
 
-        def load_x(j):
-            for c in range(2):
-                nc.sync.dma_start(out=xr[j][c][:], in_=x_v[:, j, 1024 * c:1024 * (c + 1)])
+        def load_x(j, pieces):
+            step = D_IN // pieces
+            for c in range(pieces):
+                nc.sync.dma_start(out=xr[j][:, step * c:step * (c + 1)],
+                                  in_=x_v[:, j, step * c:step * (c + 1)])
 
         def load_w(m):
             nc.sync.dma_start(out=wr[m][:], in_=w[P * m:P * (m + 1), :])
 
-        load_x(0)
-        load_x(1)
+        load_x(0, 2)
         for m in range(4):
             load_w(m)
-        load_x(2)
-        load_x(3)
+        load_x(1, 1)
+        load_x(2, 1)
+        load_x(3, 1)
         for m in range(4, HEADS):
             load_w(m)
 
@@ -72,10 +75,10 @@ def tile_attention_pa_kernel(tc, x, w, out):
 
         dummy(6)
 
-        ident = const.tile([P, P], F32, name="ident")
-        make_identity(nc, ident[:])
         idx_i = const.tile([P, NJ], I32, name="idx_i")
         nc.gpsimd.iota(idx_i[:], pattern=[[1, NJ]], base=0, channel_multiplier=NJ)
+        ident = const.tile([P, P], F32, name="ident")
+        make_identity(nc, ident[:])
 
         dm = const.tile([P, 2], F32, name="dm")
         nc.vector.memset(dm[:], 0.0)
@@ -136,23 +139,40 @@ def tile_attention_pa_kernel(tc, x, w, out):
         xg = keep.tile([P, NJ, NG, P, 2], F32, name="xg", align_bytes=64)
         xc = keep.tile([P, NJ, NG, P], U32, name="xc", align_bytes=64)
         xs = keep.tile([P, NJ, NG, P], U8, name="xs", align_bytes=64)
+        wg = {}
+        wc = {}
+        ws = {}
+        perm = {}
 
-        def copy_out(eng, dst, src):
+        def permute(key, src, eng):
+            t = ppool.tile([P, NG, 2, P], F32, name="wp")
+            perm[key] = t
+            view = src[:].bitcast(F32).rearrange("p (g q u) -> p g u q", g=NG, u=2)
             if eng == "s":
-                nc.scalar.copy(out=dst, in_=src)
+                nc.scalar.copy(out=t[:], in_=view)
             else:
-                nc.vector.tensor_copy(out=dst, in_=src)
+                nc.vector.tensor_copy(out=t[:], in_=view)
 
-        def t_x(j, engs):
+        def t_tile(key, src, dst, engs):
             for gp in range(2):
-                words = xr[j][gp][:].bitcast(F32)
                 bank = ps_t.tile([P, 2, 2, P], F32, name="tbank")
                 for gg in range(2):
+                    g = 2 * gp + gg
                     for u in range(2):
-                        nc.tensor.transpose(bank[:, gg, u, :],
-                                            words[:, 256 * gg + u:256 * (gg + 1):2], ident[:])
-                copy_out(engs[gp], xg[:, j, 2 * gp:2 * gp + 2, :, :],
-                         bank.rearrange("p g u r -> p g r u"))
+                        if key in perm:
+                            in_ap = perm[key][:, g, u, :]
+                        else:
+                            in_ap = src[:].bitcast(F32)[:, 256 * g + u:256 * (g + 1):2]
+                        nc.tensor.transpose(bank[:, gg, u, :], in_ap, ident[:])
+                o = dst[:, 2 * gp:2 * gp + 2, :, :]
+                i = bank.rearrange("p g u r -> p g r u")
+                if engs[gp] == "s":
+                    nc.scalar.copy(out=o, in_=i)
+                else:
+                    nc.vector.tensor_copy(out=o, in_=i)
+
+        def t_x(j, engs):
+            t_tile(("x", j), xr[j], xg[:, j], engs)
 
         def q_x(j):
             nc.vector.quantize_mx(
@@ -160,28 +180,16 @@ def tile_attention_pa_kernel(tc, x, w, out):
                 scales=xs[:, j].rearrange("p g r -> p (g r)"),
                 in_=xg[:, j].rearrange("p g r u -> p (g r u)").bitcast(BF16))
 
-        wg = {}
-        wc = {}
-        ws = {}
-
         def t_w(n, hlf, engs, warm=0):
             if hlf == 0:
                 wg[n] = wpool.tile([P, NG, 512, 2], F32, name="wg", align_bytes=64)
                 wc[n] = wpool.tile([P, NG, 512], U32, name="wc", align_bytes=64)
                 ws[n] = wpool.tile([P, NG, 512], U8, name="ws", align_bytes=64)
-            for g in range(NG):
-                bank = ps_t.tile([P, 2, 2, P], F32, name="tbank")
-                for mm in range(2):
-                    words = wr[4 * n + 2 * hlf + mm][:].bitcast(F32)
-                    for u in range(2):
-                        nc.tensor.transpose(bank[:, mm, u, :],
-                                            words[:, 256 * g + u:256 * (g + 1):2], ident[:])
-                dst = wg[n][:, g, 256 * hlf:256 * (hlf + 1), :]
-                copy_out(engs[g], dst.rearrange("p (m d) u -> p m d u", m=2),
-                         bank.rearrange("p m u d -> p m d u"))
-                if g == 1 and warm >= 1:
-                    dummy(1)
-                if g == 3 and warm >= 2:
+            for c in range(2):
+                m4 = 2 * hlf + c
+                t_tile(("w", 4 * n + m4), wr[4 * n + m4],
+                       wg[n][:, :, P * m4:P * (m4 + 1), :], engs[2 * c:2 * c + 2])
+                if c < warm:
                     dummy(1)
 
         def q_w(n, hlf):
@@ -193,66 +201,87 @@ def tile_attention_pa_kernel(tc, x, w, out):
                     in_=wg[n][:, g, cols, :].rearrange("p f u -> p (f u)").bitcast(BF16))
 
         acc = {}
+        res = {}
         out_v = out.rearrange("h (r j) d -> r h j d", j=NJ)
 
-        def mm(n, jp):
-            for jj in range(2):
-                j = 2 * jp + jj
-                a = ps_a.tile([P, 512], F32, name="acc")
-                acc[(n, j)] = a
-                for g in range(NG):
-                    nc.tensor.matmul_mx(out=a[:], lhsT=xc[:, j, g, :].bitcast(E5X4),
-                                        lhsT_scale=xs[:, j, g, :],
-                                        rhs=wc[n][:, g, :].bitcast(E4X4),
-                                        rhs_scale=ws[n][:, g, :],
-                                        start=(g == 0), stop=(g == NG - 1))
+        def mm(n, j):
+            a = ps_a.tile([P, 512], F32, name="acc")
+            acc[(n, j)] = a
+            for g in range(NG):
+                nc.tensor.matmul_mx(out=a[:], lhsT=xc[:, j, g, :].bitcast(E5X4),
+                                    lhsT_scale=xs[:, j, g, :],
+                                    rhs=wc[n][:, g, :].bitcast(E4X4),
+                                    rhs_scale=ws[n][:, g, :],
+                                    start=(g == 0), stop=(g == NG - 1))
 
-        def rope(n, jp, adders, split_store):
-            res = ep.tile([P, 4, 2, DH], F32, name="res")
-            for jj in range(2):
-                j = 2 * jp + jj
-                a4 = acc[(n, j)].rearrange("p (h n e) -> p h n e", h=4, e=2)
-                t1 = ep.tile([P, 4, 64, 2], F32, name="t1")
-                t2 = ep.tile([P, 4, 64, 2], F32, name="t2")
-                nc.vector.tensor_tensor(out=t1[:], in0=a4,
-                                        in1=cos2[:, j].unsqueeze(1).to_broadcast([P, 4, 64, 2]),
-                                        op=ALU.mult)
-                nc.vector.tensor_tensor(out=t2[:], in0=a4[:, :, :, ::-1],
-                                        in1=sin2[:, j].unsqueeze(1).to_broadcast([P, 4, 64, 2]),
-                                        op=ALU.mult)
-                add_eng = nc.gpsimd if adders[jj] == "g" else nc.vector
-                add_eng.tensor_tensor(out=res[:, :, jj, :],
-                                      in0=t1.rearrange("p h n e -> p h (n e)"),
-                                      in1=t2.rearrange("p h n e -> p h (n e)"), op=ALU.add)
-                if split_store:
-                    nc.sync.dma_start(out=out_v[:, 4 * n:4 * n + 4, j, :], in_=res[:, :, jj, :])
-            if not split_store:
-                nc.sync.dma_start(out=out_v[:, 4 * n:4 * n + 4, 2 * jp:2 * jp + 2, :], in_=res[:])
+        def rope(n, j, adder, split_store):
+            jp = j // 2
+            jj = j % 2
+            if jj == 0:
+                res[(n, jp)] = ep.tile([P, 4, 2, DH], F32, name="res")
+            r = res[(n, jp)]
+            a4 = acc[(n, j)].rearrange("p (h n e) -> p h n e", h=4, e=2)
+            t1 = ep.tile([P, 4, 64, 2], F32, name="t1")
+            t2 = ep.tile([P, 4, 64, 2], F32, name="t2")
+            nc.vector.tensor_tensor(out=t1[:], in0=a4,
+                                    in1=cos2[:, j].unsqueeze(1).to_broadcast([P, 4, 64, 2]),
+                                    op=ALU.mult)
+            nc.vector.tensor_tensor(out=t2[:], in0=a4[:, :, :, ::-1],
+                                    in1=sin2[:, j].unsqueeze(1).to_broadcast([P, 4, 64, 2]),
+                                    op=ALU.mult)
+            add_eng = nc.gpsimd if adder == "g" else nc.vector
+            add_eng.tensor_tensor(out=r[:, :, jj, :],
+                                  in0=t1.rearrange("p h n e -> p h (n e)"),
+                                  in1=t2.rearrange("p h n e -> p h (n e)"), op=ALU.add)
+            if split_store:
+                nc.sync.dma_start(out=out_v[:, 4 * n:4 * n + 4, j, :], in_=r[:, :, jj, :])
+            elif jj == 1:
+                nc.sync.dma_start(out=out_v[:, 4 * n:4 * n + 4, 2 * jp:2 * jp + 2, :], in_=r[:])
+
+        runs = [[("x", 2), ("x", 3)]] + [[("w", m), ("w", m + 1)] for m in range(4, HEADS, 2)]
+        plan = {("x", 2): ("s", 1), ("w", 5): ("s", 1), ("w", 7): ("v", 1), ("w", 8): ("s", 2),
+                ("w", 9): ("v", 1), ("w", 10): ("s", 2), ("w", 11): ("v", 1), ("w", 12): ("s", 2),
+                ("w", 13): ("s", 1), ("w", 15): ("s", 1)}
+
+        def permutes_at(slot):
+            for ri in range(len(runs)):
+                for key in runs[ri]:
+                    if key in plan and max(ri - plan[key][1], -1) == slot:
+                        permute(key, xr[key[1]] if key[0] == "x" else wr[key[1]], plan[key][0])
+
+        def do_run(ri):
+            if ri == 0:
+                t_x(2, "ss")
+                t_x(3, "ss")
+                permutes_at(0)
+                q_x(2)
+                q_x(3)
+            else:
+                n = 1 + (ri - 1) // 2
+                hlf = (ri - 1) % 2
+                t_w(n, hlf, "ssss")
+                permutes_at(ri)
+                q_w(n, hlf)
 
         t_x(0, "ss")
-        dummy(2)
-        t_x(1, "ss")
-        dummy(1)
         table_scalar()
         q_x(0)
+        t_w(0, 0, "sssv")
+        q_w(0, 0)
+        t_w(0, 1, "sssv")
+        q_w(0, 1)
+        t_x(1, "sv")
         q_x(1)
         table_expand()
-        t_w(0, 0, "sssv", 2)
-        q_w(0, 0)
-        t_w(0, 1, "sssv", 2)
-        q_w(0, 1)
-        t_x(2, "ss")
-        dummy(1)
-        t_x(3, "sv")
-        dummy(1)
-        q_x(2)
-        q_x(3)
-        t_w(1, 0, "sssv", 1)
-        q_w(1, 0)
-        t_list = [(1, 1), (2, 0), (2, 1), (3, 0), (3, 1)]
-        for k in range(8):
-            mm(k // 2, k % 2)
-            rope(k // 2, k % 2, "gv" if k == 7 else "gg", k == 7)
-            if k < len(t_list):
-                t_w(t_list[k][0], t_list[k][1], "ssss")
-                q_w(t_list[k][0], t_list[k][1])
+        permutes_at(-1)
+        units = [1, 1, 1, 1, 2, 2, 2, 2, 2, 2]
+        b = 0
+        for ui in range(len(units)):
+            banks = list(range(b, b + units[ui]))
+            b += units[ui]
+            for bb in banks:
+                mm(bb // 4, bb % 4)
+            for bb in banks:
+                rope(bb // 4, bb % 4, "v" if bb == 15 else "g", bb >= 14)
+            if ui < len(runs):
+                do_run(ui)

@@ -34,36 +34,33 @@ def tile_attention_pa_kernel(tc, x, w, out):
         keep = ctx.enter_context(tc.tile_pool(name="keep", bufs=1))
         wpool = ctx.enter_context(tc.tile_pool(name="wpool", bufs=2))
         ep = ctx.enter_context(tc.tile_pool(name="ep", bufs=3))
-        ppool = ctx.enter_context(tc.tile_pool(name="ppool", bufs=4))
+        ppool = ctx.enter_context(tc.tile_pool(name="ppool", bufs=6))
         ps_t = ctx.enter_context(tc.psum_pool(name="ps_t", bufs=4))
         ps_a = ctx.enter_context(tc.psum_pool(name="ps_a", bufs=4))
         ctx.enter_context(tc.manual_schedule())
 
         x_v = x.rearrange("(r j) k -> r j k", j=NJ)
-        xr = []
-        wr = []
-        for j in range(NJ):
-            xr.append(raw.tile([P, D_IN], BF16, name="xr%d" % j))
-        for m in range(HEADS):
-            wr.append(raw.tile([P, D_IN], BF16, name="wr%d" % m))
+        xr = [[raw.tile([P, 1024], BF16, name="xr%d_%d" % (j, c)) for c in range(2)] for j in range(NJ)]
+        wr = [[raw.tile([P, 1024], BF16, name="wr%d_%d" % (m, c)) for c in range(2)]
+              for m in range(HEADS)]
 
-        def load_x(j, pieces):
-            step = D_IN // pieces
-            for c in range(pieces):
-                nc.sync.dma_start(out=xr[j][:, step * c:step * (c + 1)],
-                                  in_=x_v[:, j, step * c:step * (c + 1)])
+        def load_x(j):
+            for c in range(2):
+                nc.sync.dma_start(out=xr[j][c][:], in_=x_v[:, j, 1024 * c:1024 * (c + 1)])
 
-        def load_w(m):
-            nc.sync.dma_start(out=wr[m][:], in_=w[P * m:P * (m + 1), :])
+        def load_w_group(n):
+            for c in range(2):
+                for m in range(4 * n, 4 * n + 4):
+                    nc.sync.dma_start(out=wr[m][c][:],
+                                      in_=w[P * m:P * (m + 1), 1024 * c:1024 * (c + 1)])
 
-        load_x(0, 2)
-        for m in range(4):
-            load_w(m)
-        load_x(1, 1)
-        load_x(2, 1)
-        load_x(3, 1)
-        for m in range(4, HEADS):
-            load_w(m)
+        load_x(0)
+        load_w_group(0)
+        load_x(1)
+        load_x(2)
+        load_x(3)
+        for n in range(1, NGRP):
+            load_w_group(n)
 
         dz = const.tile([P, 512], BF16, name="dz")
         nc.vector.memset(dz[:], 0.0)
@@ -144,61 +141,63 @@ def tile_attention_pa_kernel(tc, x, w, out):
         ws = {}
         perm = {}
 
-        def permute(key, src, eng):
-            t = ppool.tile([P, NG, 2, P], F32, name="wp")
+        def half_of(key):
+            return xr[key[1]][key[2]] if key[0] == "x" else wr[key[1]][key[2]]
+
+        def permute(key):
+            t = ppool.tile([P, 2, 2, P], F32, name="wp")
             perm[key] = t
-            view = src[:].bitcast(F32).rearrange("p (g q u) -> p g u q", g=NG, u=2)
+            nc.scalar.copy(out=t[:], in_=half_of(key)[:].bitcast(F32).rearrange(
+                "p (g q u) -> p g u q", g=2, u=2))
+
+        def t_bank(key, dst, eng):
+            c = key[2]
+            bank = ps_t.tile([P, 2, 2, P], F32, name="tbank")
+            for gg in range(2):
+                for u in range(2):
+                    if key in perm:
+                        in_ap = perm[key][:, gg, u, :]
+                    else:
+                        in_ap = half_of(key)[:].bitcast(F32)[:, 256 * gg + u:256 * (gg + 1):2]
+                    nc.tensor.transpose(bank[:, gg, u, :], in_ap, ident[:])
+            o = dst[:, 2 * c:2 * c + 2, :, :]
+            i = bank.rearrange("p g u r -> p g r u")
             if eng == "s":
-                nc.scalar.copy(out=t[:], in_=view)
+                nc.scalar.copy(out=o, in_=i)
             else:
-                nc.vector.tensor_copy(out=t[:], in_=view)
+                nc.vector.tensor_copy(out=o, in_=i)
 
-        def t_tile(key, src, dst, engs):
-            for gp in range(2):
-                bank = ps_t.tile([P, 2, 2, P], F32, name="tbank")
-                for gg in range(2):
-                    g = 2 * gp + gg
-                    for u in range(2):
-                        if key in perm:
-                            in_ap = perm[key][:, g, u, :]
-                        else:
-                            in_ap = src[:].bitcast(F32)[:, 256 * g + u:256 * (g + 1):2]
-                        nc.tensor.transpose(bank[:, gg, u, :], in_ap, ident[:])
-                o = dst[:, 2 * gp:2 * gp + 2, :, :]
-                i = bank.rearrange("p g u r -> p g r u")
-                if engs[gp] == "s":
-                    nc.scalar.copy(out=o, in_=i)
-                else:
-                    nc.vector.tensor_copy(out=o, in_=i)
-
-        def t_x(j, engs):
-            t_tile(("x", j), xr[j], xg[:, j], engs)
-
-        def q_x(j):
+        def q_x(j0, j1):
             nc.vector.quantize_mx(
-                out=xc[:, j].rearrange("p g r -> p (g r)").bitcast(E5X4),
-                scales=xs[:, j].rearrange("p g r -> p (g r)"),
-                in_=xg[:, j].rearrange("p g r u -> p (g r u)").bitcast(BF16))
+                out=xc[:, j0:j1].rearrange("p j g r -> p (j g r)").bitcast(E5X4),
+                scales=xs[:, j0:j1].rearrange("p j g r -> p (j g r)"),
+                in_=xg[:, j0:j1].rearrange("p j g r u -> p (j g r u)").bitcast(BF16))
 
-        def t_w(n, hlf, engs, warm=0):
-            if hlf == 0:
-                wg[n] = wpool.tile([P, NG, 512, 2], F32, name="wg", align_bytes=64)
-                wc[n] = wpool.tile([P, NG, 512], U32, name="wc", align_bytes=64)
-                ws[n] = wpool.tile([P, NG, 512], U8, name="ws", align_bytes=64)
-            for c in range(2):
-                m4 = 2 * hlf + c
-                t_tile(("w", 4 * n + m4), wr[4 * n + m4],
-                       wg[n][:, :, P * m4:P * (m4 + 1), :], engs[2 * c:2 * c + 2])
-                if c < warm:
-                    dummy(1)
+        def q_w(n, c):
+            nc.vector.quantize_mx(
+                out=wc[n][:, 2 * c:2 * c + 2, :].rearrange("p g f -> p (g f)").bitcast(E4X4),
+                scales=ws[n][:, 2 * c:2 * c + 2, :].rearrange("p g f -> p (g f)"),
+                in_=wg[n][:, 2 * c:2 * c + 2, :, :].rearrange("p g f u -> p (g f u)").bitcast(BF16))
 
-        def q_w(n, hlf):
-            cols = slice(256 * hlf, 256 * (hlf + 1))
-            for g in range(NG):
-                nc.vector.quantize_mx(
-                    out=wc[n][:, g, cols].bitcast(E4X4),
-                    scales=ws[n][:, g, cols],
-                    in_=wg[n][:, g, cols, :].rearrange("p f u -> p (f u)").bitcast(BF16))
+        def run_keys(ri):
+            if ri == 0:
+                return [("x", 2, 0), ("x", 2, 1), ("x", 3, 0), ("x", 3, 1)]
+            n = 1 + (ri - 1) // 2
+            return [("w", 4 * n + m4, (ri - 1) % 2) for m4 in range(4)]
+
+        def t_run(keys, engs):
+            for k in range(4):
+                key = keys[k]
+                if key[0] == "x":
+                    t_bank(key, xg[:, key[1]], engs[k])
+                else:
+                    n = key[1] // 4
+                    m4 = key[1] % 4
+                    if n not in wg:
+                        wg[n] = wpool.tile([P, NG, 512, 2], F32, name="wg", align_bytes=64)
+                        wc[n] = wpool.tile([P, NG, 512], U32, name="wc", align_bytes=64)
+                        ws[n] = wpool.tile([P, NG, 512], U8, name="ws", align_bytes=64)
+                    t_bank(key, wg[n][:, :, P * m4:P * (m4 + 1), :], engs[k])
 
         acc = {}
         res = {}
@@ -223,12 +222,12 @@ def tile_attention_pa_kernel(tc, x, w, out):
             a4 = acc[(n, j)].rearrange("p (h n e) -> p h n e", h=4, e=2)
             t1 = ep.tile([P, 4, 64, 2], F32, name="t1")
             t2 = ep.tile([P, 4, 64, 2], F32, name="t2")
-            nc.vector.tensor_tensor(out=t1[:], in0=a4,
-                                    in1=cos2[:, j].unsqueeze(1).to_broadcast([P, 4, 64, 2]),
-                                    op=ALU.mult)
-            nc.vector.tensor_tensor(out=t2[:], in0=a4[:, :, :, ::-1],
-                                    in1=sin2[:, j].unsqueeze(1).to_broadcast([P, 4, 64, 2]),
-                                    op=ALU.mult)
+            nc.vector.tensor_tensor(out=t1[:],
+                                    in0=cos2[:, j].unsqueeze(1).to_broadcast([P, 4, 64, 2]),
+                                    in1=a4, op=ALU.mult)
+            nc.vector.tensor_tensor(out=t2[:],
+                                    in0=sin2[:, j].unsqueeze(1).to_broadcast([P, 4, 64, 2]),
+                                    in1=a4[:, :, :, ::-1], op=ALU.mult)
             add_eng = nc.gpsimd if adder == "g" else nc.vector
             add_eng.tensor_tensor(out=r[:, :, jj, :],
                                   in0=t1.rearrange("p h n e -> p h (n e)"),
@@ -238,42 +237,36 @@ def tile_attention_pa_kernel(tc, x, w, out):
             elif jj == 1:
                 nc.sync.dma_start(out=out_v[:, 4 * n:4 * n + 4, 2 * jp:2 * jp + 2, :], in_=r[:])
 
-        runs = [[("x", 2), ("x", 3)]] + [[("w", m), ("w", m + 1)] for m in range(4, HEADS, 2)]
-        plan = {("x", 2): ("s", 1), ("w", 5): ("s", 1), ("w", 7): ("v", 1), ("w", 8): ("s", 2),
-                ("w", 9): ("v", 1), ("w", 10): ("s", 2), ("w", 11): ("v", 1), ("w", 12): ("s", 2),
-                ("w", 13): ("s", 1), ("w", 15): ("s", 1)}
+        N_RUNS = 7
 
-        def permutes_at(slot):
-            for ri in range(len(runs)):
-                for key in runs[ri]:
-                    if key in plan and max(ri - plan[key][1], -1) == slot:
-                        permute(key, xr[key[1]] if key[0] == "x" else wr[key[1]], plan[key][0])
+        def permuted_banks(ri):
+            return 2
+
+        def permutes_for(ri):
+            if ri < N_RUNS:
+                for key in run_keys(ri)[4 - permuted_banks(ri):]:
+                    permute(key)
 
         def do_run(ri):
+            t_run(run_keys(ri), "ssss")
+            permutes_for(ri + 1)
             if ri == 0:
-                t_x(2, "ss")
-                t_x(3, "ss")
-                permutes_at(0)
-                q_x(2)
-                q_x(3)
+                q_x(2, 4)
             else:
-                n = 1 + (ri - 1) // 2
-                hlf = (ri - 1) % 2
-                t_w(n, hlf, "ssss")
-                permutes_at(ri)
-                q_w(n, hlf)
+                q_w(1 + (ri - 1) // 2, (ri - 1) % 2)
 
-        t_x(0, "ss")
+        t_bank(("x", 0, 0), xg[:, 0], "s")
+        t_bank(("x", 0, 1), xg[:, 0], "s")
         table_scalar()
-        q_x(0)
-        t_w(0, 0, "sssv")
-        q_w(0, 0)
-        t_w(0, 1, "sssv")
-        q_w(0, 1)
-        t_x(1, "sv")
-        q_x(1)
+        q_x(0, 1)
+        for c in range(2):
+            t_run([("w", m4, c) for m4 in range(4)], "sssv")
+            q_w(0, c)
+        t_bank(("x", 1, 0), xg[:, 1], "s")
+        t_bank(("x", 1, 1), xg[:, 1], "v")
+        q_x(1, 2)
         table_expand()
-        permutes_at(-1)
+        permutes_for(0)
         units = [1, 1, 1, 1, 2, 2, 2, 2, 2, 2]
         b = 0
         for ui in range(len(units)):
@@ -283,5 +276,5 @@ def tile_attention_pa_kernel(tc, x, w, out):
                 mm(bb // 4, bb % 4)
             for bb in banks:
                 rope(bb // 4, bb % 4, "v" if bb == 15 else "g", bb >= 14)
-            if ui < len(runs):
+            if ui < N_RUNS:
                 do_run(ui)

@@ -34,43 +34,36 @@ def tile_attention_pa_kernel(tc, x, w, out):
         keep = ctx.enter_context(tc.tile_pool(name="keep", bufs=1))
         wpool = ctx.enter_context(tc.tile_pool(name="wpool", bufs=2))
         ep = ctx.enter_context(tc.tile_pool(name="ep", bufs=3))
-        ppool = ctx.enter_context(tc.tile_pool(name="ppool", bufs=6))
+        ppool = ctx.enter_context(tc.tile_pool(name="ppool", bufs=4))
         ps_t = ctx.enter_context(tc.psum_pool(name="ps_t", bufs=4))
         ps_a = ctx.enter_context(tc.psum_pool(name="ps_a", bufs=4))
         ctx.enter_context(tc.manual_schedule())
 
         x_v = x.rearrange("(r j) k -> r j k", j=NJ)
-        xr = [[raw.tile([P, 1024], BF16, name="xr%d_%d" % (j, c)) for c in range(2)] for j in range(NJ)]
-        wr = [[raw.tile([P, 1024], BF16, name="wr%d_%d" % (m, c)) for c in range(2)]
-              for m in range(HEADS)]
+        xr = []
+        wr = []
+        for j in range(NJ):
+            xr.append(raw.tile([P, D_IN], BF16, name="xr%d" % j))
+        for m in range(HEADS):
+            wr.append(raw.tile([P, D_IN], BF16, name="wr%d" % m))
 
-        def load_x(j):
-            for c in range(2):
-                nc.sync.dma_start(out=xr[j][c][:], in_=x_v[:, j, 1024 * c:1024 * (c + 1)])
+        def load_x(j, pieces):
+            step = D_IN // pieces
+            for c in range(pieces):
+                nc.sync.dma_start(out=xr[j][:, step * c:step * (c + 1)],
+                                  in_=x_v[:, j, step * c:step * (c + 1)])
 
-        def load_w_group(n):
-            for c in range(2):
-                for m in range(4 * n, 4 * n + 4):
-                    nc.sync.dma_start(out=wr[m][c][:],
-                                      in_=w[P * m:P * (m + 1), 1024 * c:1024 * (c + 1)])
+        def load_w(m):
+            nc.sync.dma_start(out=wr[m][:], in_=w[P * m:P * (m + 1), :])
 
-        load_x(0)
-        load_w_group(0)
-        load_x(1)
-        load_x(2)
-        load_x(3)
-        for n in range(1, NGRP):
-            load_w_group(n)
-
-        dz = const.tile([P, 512], BF16, name="dz")
-        nc.vector.memset(dz[:], 0.0)
-        dacc = ps_a.tile([P, 512], F32, name="acc")
-
-        def dummy(count):
-            for i in range(count):
-                nc.tensor.matmul(out=dacc[:], lhsT=dz[:, 0:P], rhs=dz[:], start=True, stop=True)
-
-        dummy(6)
+        load_x(0, 2)
+        for m in range(4):
+            load_w(m)
+        load_x(1, 1)
+        load_x(2, 1)
+        load_x(3, 1)
+        for m in range(4, HEADS):
+            load_w(m)
 
         idx_i = const.tile([P, NJ], I32, name="idx_i")
         nc.gpsimd.iota(idx_i[:], pattern=[[1, NJ]], base=0, channel_multiplier=NJ)
@@ -125,13 +118,11 @@ def tile_attention_pa_kernel(tc, x, w, out):
             nc.scalar.activation(out=sin_t[:], in_=r4[:], func=ACT.Sin)
             nc.scalar.activation(out=cos_t[:], in_=ab[:], func=ACT.Sin, bias=math.pi / 2.0,
                                  scale=-1.0)
-
-        def table_expand():
-            nc.vector.tensor_copy(out=cos2[:, :, :, 0], in_=cos_t[:])
-            nc.vector.tensor_copy(out=cos2[:, :, :, 1], in_=cos_t[:])
-            nc.vector.tensor_scalar(out=sin2[:, :, :, 0], in0=sin_t[:], scalar1=-1.0,
-                                    scalar2=None, op0=ALU.mult)
-            nc.vector.tensor_copy(out=sin2[:, :, :, 1], in_=sin_t[:])
+            for e in range(2):
+                nc.gpsimd.tensor_scalar(out=cos2[:, :, :, e], in0=cos_t[:], scalar1=1.0,
+                                        scalar2=0.0, op0=ALU.mult, op1=ALU.add)
+                nc.gpsimd.tensor_scalar(out=sin2[:, :, :, e], in0=sin_t[:], scalar1=2.0 * e - 1.0,
+                                        scalar2=0.0, op0=ALU.mult, op1=ALU.add)
 
         xg = keep.tile([P, NJ, NG, P, 2], F32, name="xg", align_bytes=64)
         xc = keep.tile([P, NJ, NG, P], U32, name="xc", align_bytes=64)
@@ -141,63 +132,61 @@ def tile_attention_pa_kernel(tc, x, w, out):
         ws = {}
         perm = {}
 
-        def half_of(key):
-            return xr[key[1]][key[2]] if key[0] == "x" else wr[key[1]][key[2]]
-
-        def permute(key):
-            t = ppool.tile([P, 2, 2, P], F32, name="wp")
+        def permute(key, src, eng):
+            t = ppool.tile([P, NG, 2, P], F32, name="wp")
             perm[key] = t
-            nc.scalar.copy(out=t[:], in_=half_of(key)[:].bitcast(F32).rearrange(
-                "p (g q u) -> p g u q", g=2, u=2))
-
-        def t_bank(key, dst, eng):
-            c = key[2]
-            bank = ps_t.tile([P, 2, 2, P], F32, name="tbank")
-            for gg in range(2):
-                for u in range(2):
-                    if key in perm:
-                        in_ap = perm[key][:, gg, u, :]
-                    else:
-                        in_ap = half_of(key)[:].bitcast(F32)[:, 256 * gg + u:256 * (gg + 1):2]
-                    nc.tensor.transpose(bank[:, gg, u, :], in_ap, ident[:])
-            o = dst[:, 2 * c:2 * c + 2, :, :]
-            i = bank.rearrange("p g u r -> p g r u")
+            view = src[:].bitcast(F32).rearrange("p (g q u) -> p g u q", g=NG, u=2)
             if eng == "s":
-                nc.scalar.copy(out=o, in_=i)
+                nc.scalar.copy(out=t[:], in_=view)
             else:
-                nc.vector.tensor_copy(out=o, in_=i)
+                nc.vector.tensor_copy(out=t[:], in_=view)
 
-        def q_x(j0, j1):
-            nc.vector.quantize_mx(
-                out=xc[:, j0:j1].rearrange("p j g r -> p (j g r)").bitcast(E5X4),
-                scales=xs[:, j0:j1].rearrange("p j g r -> p (j g r)"),
-                in_=xg[:, j0:j1].rearrange("p j g r u -> p (j g r u)").bitcast(BF16))
-
-        def q_w(n, c):
-            nc.vector.quantize_mx(
-                out=wc[n][:, 2 * c:2 * c + 2, :].rearrange("p g f -> p (g f)").bitcast(E4X4),
-                scales=ws[n][:, 2 * c:2 * c + 2, :].rearrange("p g f -> p (g f)"),
-                in_=wg[n][:, 2 * c:2 * c + 2, :, :].rearrange("p g f u -> p (g f u)").bitcast(BF16))
-
-        def run_keys(ri):
-            if ri == 0:
-                return [("x", 2, 0), ("x", 2, 1), ("x", 3, 0), ("x", 3, 1)]
-            n = 1 + (ri - 1) // 2
-            return [("w", 4 * n + m4, (ri - 1) % 2) for m4 in range(4)]
-
-        def t_run(keys, engs):
-            for k in range(4):
-                key = keys[k]
-                if key[0] == "x":
-                    t_bank(key, xg[:, key[1]], engs[k])
+        def t_tile(key, src, dst, engs):
+            for gp in range(2):
+                bank = ps_t.tile([P, 2, 2, P], F32, name="tbank")
+                for gg in range(2):
+                    g = 2 * gp + gg
+                    for u in range(2):
+                        if key in perm:
+                            in_ap = perm[key][:, g, u, :]
+                        else:
+                            in_ap = src[:].bitcast(F32)[:, 256 * g + u:256 * (g + 1):2]
+                        nc.tensor.transpose(bank[:, gg, u, :], in_ap, ident[:])
+                o = dst[:, 2 * gp:2 * gp + 2, :, :]
+                i = bank.rearrange("p g u r -> p g r u")
+                if engs[gp] == "s":
+                    nc.scalar.copy(out=o, in_=i)
                 else:
-                    n = key[1] // 4
-                    m4 = key[1] % 4
-                    if n not in wg:
-                        wg[n] = wpool.tile([P, NG, 512, 2], F32, name="wg", align_bytes=64)
-                        wc[n] = wpool.tile([P, NG, 512], U32, name="wc", align_bytes=64)
-                        ws[n] = wpool.tile([P, NG, 512], U8, name="ws", align_bytes=64)
-                    t_bank(key, wg[n][:, :, P * m4:P * (m4 + 1), :], engs[k])
+                    nc.vector.tensor_copy(out=o, in_=i)
+
+        def t_x(j, engs):
+            t_tile(("x", j), xr[j], xg[:, j], engs)
+
+        def q_x(j):
+            nc.vector.quantize_mx(
+                out=xc[:, j].rearrange("p g r -> p (g r)").bitcast(E5X4),
+                scales=xs[:, j].rearrange("p g r -> p (g r)"),
+                in_=xg[:, j].rearrange("p g r u -> p (g r u)").bitcast(BF16))
+
+        def t_w(n, hlf, engs, between=None):
+            if hlf == 0:
+                wg[n] = wpool.tile([P, NG, 512, 2], F32, name="wg", align_bytes=64)
+                wc[n] = wpool.tile([P, NG, 512], U32, name="wc", align_bytes=64)
+                ws[n] = wpool.tile([P, NG, 512], U8, name="ws", align_bytes=64)
+            for c in range(2):
+                m4 = 2 * hlf + c
+                t_tile(("w", 4 * n + m4), wr[4 * n + m4],
+                       wg[n][:, :, P * m4:P * (m4 + 1), :], engs[2 * c:2 * c + 2])
+                if c == 0 and between is not None:
+                    between()
+
+        def q_w(n, hlf):
+            cols = slice(256 * hlf, 256 * (hlf + 1))
+            for g in range(NG):
+                nc.vector.quantize_mx(
+                    out=wc[n][:, g, cols].bitcast(E4X4),
+                    scales=ws[n][:, g, cols],
+                    in_=wg[n][:, g, cols, :].rearrange("p f u -> p (f u)").bitcast(BF16))
 
         acc = {}
         res = {}
@@ -222,12 +211,12 @@ def tile_attention_pa_kernel(tc, x, w, out):
             a4 = acc[(n, j)].rearrange("p (h n e) -> p h n e", h=4, e=2)
             t1 = ep.tile([P, 4, 64, 2], F32, name="t1")
             t2 = ep.tile([P, 4, 64, 2], F32, name="t2")
-            nc.vector.tensor_tensor(out=t1[:],
-                                    in0=cos2[:, j].unsqueeze(1).to_broadcast([P, 4, 64, 2]),
-                                    in1=a4, op=ALU.mult)
-            nc.vector.tensor_tensor(out=t2[:],
-                                    in0=sin2[:, j].unsqueeze(1).to_broadcast([P, 4, 64, 2]),
-                                    in1=a4[:, :, :, ::-1], op=ALU.mult)
+            nc.vector.tensor_tensor(out=t1[:], in0=a4,
+                                    in1=cos2[:, j].unsqueeze(1).to_broadcast([P, 4, 64, 2]),
+                                    op=ALU.mult)
+            nc.vector.tensor_tensor(out=t2[:], in0=a4[:, :, :, ::-1],
+                                    in1=sin2[:, j].unsqueeze(1).to_broadcast([P, 4, 64, 2]),
+                                    op=ALU.mult)
             add_eng = nc.gpsimd if adder == "g" else nc.vector
             add_eng.tensor_tensor(out=r[:, :, jj, :],
                                   in0=t1.rearrange("p h n e -> p h (n e)"),
@@ -237,36 +226,40 @@ def tile_attention_pa_kernel(tc, x, w, out):
             elif jj == 1:
                 nc.sync.dma_start(out=out_v[:, 4 * n:4 * n + 4, 2 * jp:2 * jp + 2, :], in_=r[:])
 
-        N_RUNS = 7
+        runs = [[("x", 2), ("x", 3)]] + [[("w", m), ("w", m + 1)] for m in range(4, HEADS, 2)]
+        plan = {("x", 2): ("s", 1), ("w", 5): ("s", 1), ("w", 8): ("s", 2),
+                ("w", 10): ("s", 2), ("w", 12): ("s", 2),
+                ("w", 13): ("s", 1), ("w", 15): ("s", 1)}
 
-        def permuted_banks(ri):
-            return 2
-
-        def permutes_for(ri):
-            if ri < N_RUNS:
-                for key in run_keys(ri)[4 - permuted_banks(ri):]:
-                    permute(key)
+        def permutes_at(slot):
+            for ri in range(len(runs)):
+                for key in runs[ri]:
+                    if key in plan and max(ri - plan[key][1], -1) == slot:
+                        permute(key, xr[key[1]] if key[0] == "x" else wr[key[1]], plan[key][0])
 
         def do_run(ri):
-            t_run(run_keys(ri), "ssss")
-            permutes_for(ri + 1)
             if ri == 0:
-                q_x(2, 4)
+                t_x(2, "ss")
+                t_x(3, "ss")
+                permutes_at(0)
+                q_x(2)
+                q_x(3)
             else:
-                q_w(1 + (ri - 1) // 2, (ri - 1) % 2)
+                n = 1 + (ri - 1) // 2
+                hlf = (ri - 1) % 2
+                t_w(n, hlf, "ssss")
+                permutes_at(ri)
+                q_w(n, hlf)
 
-        t_bank(("x", 0, 0), xg[:, 0], "s")
-        t_bank(("x", 0, 1), xg[:, 0], "s")
-        table_scalar()
-        q_x(0, 1)
-        for c in range(2):
-            t_run([("w", m4, c) for m4 in range(4)], "sssv")
-            q_w(0, c)
-        t_bank(("x", 1, 0), xg[:, 1], "s")
-        t_bank(("x", 1, 1), xg[:, 1], "v")
-        q_x(1, 2)
-        table_expand()
-        permutes_for(0)
+        t_x(0, "ss")
+        q_x(0)
+        t_w(0, 0, "sssv", table_scalar)
+        q_w(0, 0)
+        t_w(0, 1, "sssv")
+        q_w(0, 1)
+        t_x(1, "sv")
+        q_x(1)
+        permutes_at(-1)
         units = [1, 1, 1, 1, 2, 2, 2, 2, 2, 2]
         b = 0
         for ui in range(len(units)):
@@ -276,5 +269,5 @@ def tile_attention_pa_kernel(tc, x, w, out):
                 mm(bb // 4, bb % 4)
             for bb in banks:
                 rope(bb // 4, bb % 4, "v" if bb == 15 else "g", bb >= 14)
-            if ui < N_RUNS:
+            if ui < len(runs):
                 do_run(ui)

@@ -21,9 +21,6 @@ NJ = 4
 NG = 4
 NGRP = 4
 TWO_PI = 2.0 * math.pi
-C1 = 6.28125
-C2C = 0.0019353628158569336
-C3 = TWO_PI - C1 - C2C
 
 
 def tile_attention_pa_kernel(tc, x, w, out):
@@ -76,38 +73,35 @@ def tile_attention_pa_kernel(tc, x, w, out):
 
         idx_f = const.tile([P, NJ], F32, name="idx_f")
         nc.vector.tensor_copy(out=idx_f[:], in_=idx_i[:])
-        th = const.tile([P, 64], F32, name="th")
-        nc.vector.memset(th[:, 0:1], 1.0)
+        lh = const.tile([P, 2, 8], F32, name="lh")
+        nc.vector.memset(lh[:, :, 0:1], 1.0)
         q = 10000.0 ** (-1.0 / 64.0)
-        for s in range(6):
+        for s in range(3):
             wd = 1 << s
-            nc.vector.tensor_scalar(out=th[:, wd:2 * wd], in0=th[:, 0:wd], scalar1=q ** wd,
-                                    scalar2=None, op0=ALU.mult)
-        ang = const.tile([P, NJ, 64], F32, name="ang")
+            for c in range(2):
+                nc.vector.tensor_scalar(out=lh[:, c, wd:2 * wd], in0=lh[:, c, 0:wd],
+                                        scalar1=q ** (wd * (1 + 7 * c)), scalar2=None, op0=ALU.mult)
+        hij = const.tile([P, NJ, 8], F32, name="hij")
         for j in range(NJ):
-            nc.vector.tensor_scalar(out=ang[:, j, :], in0=th[:], scalar1=idx_f[:, j:j + 1],
-                                    scalar2=None, op0=ALU.mult)
+            nc.vector.tensor_scalar(out=hij[:, j, :], in0=lh[:, 1, :], scalar1=idx_f[:, j:j + 1],
+                                    scalar2=1.0 / TWO_PI, op0=ALU.mult, op1=ALU.mult)
+        ang = const.tile([P, NJ, 64], F32, name="ang")
+        nc.vector.tensor_tensor(out=ang.rearrange("p j (a b) -> p (j a) b", b=8),
+                                in0=hij.rearrange("p j a -> p (j a)").unsqueeze(2)
+                                .to_broadcast([P, NJ * 8, 8]),
+                                in1=lh[:, 0, :].unsqueeze(1).to_broadcast([P, NJ * 8, 8]),
+                                op=ALU.mult)
         n_i = const.tile([P, NJ, 64], I32, name="n_i")
-        nc.vector.tensor_scalar(out=n_i[:], in0=ang[:], scalar1=1.0 / TWO_PI, scalar2=None,
-                                op0=ALU.mult)
+        nc.vector.tensor_copy(out=n_i[:], in_=ang[:])
         n_f = const.tile([P, NJ, 64], F32, name="n_f")
         nc.vector.tensor_copy(out=n_f[:], in_=n_i[:])
-        r1 = const.tile([P, NJ, 64], F32, name="r1")
-        nc.vector.scalar_tensor_tensor(out=r1[:], in0=n_f[:], scalar=-C1, in1=ang[:],
-                                       op0=ALU.mult, op1=ALU.add)
-        r2 = const.tile([P, NJ, 64], F32, name="r2")
-        nc.vector.scalar_tensor_tensor(out=r2[:], in0=n_f[:], scalar=-C2C, in1=r1[:],
-                                       op0=ALU.mult, op1=ALU.add)
-        r3 = const.tile([P, NJ, 64], F32, name="r3")
-        nc.vector.scalar_tensor_tensor(out=r3[:], in0=n_f[:], scalar=-C3, in1=r2[:],
-                                       op0=ALU.mult, op1=ALU.add)
-        fd = const.tile([P, NJ, 64], F32, name="fd")
-        nc.vector.tensor_scalar(out=fd[:], in0=r3[:], scalar1=math.pi, scalar2=-TWO_PI,
-                                op0=ALU.is_gt, op1=ALU.mult)
-        r4 = const.tile([P, NJ, 64], F32, name="r4")
-        nc.vector.tensor_tensor(out=r4[:], in0=r3[:], in1=fd[:], op=ALU.add)
+        fr = const.tile([P, NJ, 64], F32, name="fr")
+        nc.vector.tensor_tensor(out=fr[:], in0=ang[:], in1=n_f[:], op=ALU.subtract)
+        yn = const.tile([P, NJ, 64], F32, name="yn")
+        nc.vector.scalar_tensor_tensor(out=yn[:], in0=fr[:], scalar=0.5, in1=fr[:],
+                                       op0=ALU.is_gt, op1=ALU.subtract)
         ab = const.tile([P, NJ, 64], F32, name="ab")
-        nc.vector.scalar_tensor_tensor(out=ab[:], in0=r4[:], scalar=-1.0, in1=r4[:],
+        nc.vector.scalar_tensor_tensor(out=ab[:], in0=yn[:], scalar=-1.0, in1=yn[:],
                                        op0=ALU.mult, op1=ALU.max)
         sin_t = const.tile([P, NJ, 64], F32, name="sin_t")
         cos_t = const.tile([P, NJ, 64], F32, name="cos_t")
@@ -115,9 +109,9 @@ def tile_attention_pa_kernel(tc, x, w, out):
         sin2 = const.tile([P, NJ, 64, 2], F32, name="sin2")
 
         def table_scalar():
-            nc.scalar.activation(out=sin_t[:], in_=r4[:], func=ACT.Sin)
+            nc.scalar.activation(out=sin_t[:], in_=yn[:], func=ACT.Sin, scale=-TWO_PI)
             nc.scalar.activation(out=cos_t[:], in_=ab[:], func=ACT.Sin, bias=math.pi / 2.0,
-                                 scale=-1.0)
+                                 scale=-TWO_PI)
             for e in range(2):
                 nc.gpsimd.tensor_scalar(out=cos2[:, :, :, e], in0=cos_t[:], scalar1=1.0,
                                         scalar2=0.0, op0=ALU.mult, op1=ALU.add)

@@ -71,8 +71,6 @@ def tile_attention_pa_kernel(tc, x, w, out):
         nc.vector.memset(dm[:], 0.0)
         nc.scalar.activation(out=dm[:, 1:2], in_=dm[:, 0:1], func=ACT.Sin)
 
-        idx_f = const.tile([P, NJ], F32, name="idx_f")
-        nc.vector.tensor_copy(out=idx_f[:], in_=idx_i[:])
         lh = const.tile([P, 2, 8], F32, name="lh")
         nc.vector.memset(lh[:, :, 0:1], 1.0)
         q = 10000.0 ** (-1.0 / 64.0)
@@ -81,15 +79,17 @@ def tile_attention_pa_kernel(tc, x, w, out):
             for c in range(2):
                 nc.vector.tensor_scalar(out=lh[:, c, wd:2 * wd], in0=lh[:, c, 0:wd],
                                         scalar1=q ** (wd * (1 + 7 * c)), scalar2=None, op0=ALU.mult)
-        hij = const.tile([P, NJ, 8], F32, name="hij")
-        for j in range(NJ):
-            nc.vector.tensor_scalar(out=hij[:, j, :], in0=lh[:, 1, :], scalar1=idx_f[:, j:j + 1],
-                                    scalar2=1.0 / TWO_PI, op0=ALU.mult, op1=ALU.mult)
+        idx_s = const.tile([P, NJ], F32, name="idx_s")
+        nc.vector.tensor_scalar(out=idx_s[:], in0=idx_i[:], scalar1=1.0 / TWO_PI, scalar2=None,
+                                op0=ALU.mult)
+        th = const.tile([P, 8, 8], F32, name="th")
+        nc.vector.tensor_tensor(out=th[:], in0=lh[:, 1, :].unsqueeze(2).to_broadcast([P, 8, 8]),
+                                in1=lh[:, 0, :].unsqueeze(1).to_broadcast([P, 8, 8]),
+                                op=ALU.mult)
         ang = const.tile([P, NJ, 64], F32, name="ang")
-        nc.vector.tensor_tensor(out=ang.rearrange("p j (a b) -> p (j a) b", b=8),
-                                in0=hij.rearrange("p j a -> p (j a)").unsqueeze(2)
-                                .to_broadcast([P, NJ * 8, 8]),
-                                in1=lh[:, 0, :].unsqueeze(1).to_broadcast([P, NJ * 8, 8]),
+        nc.vector.tensor_tensor(out=ang[:], in0=idx_s[:].unsqueeze(2).to_broadcast([P, NJ, 64]),
+                                in1=th.rearrange("p a b -> p (a b)").unsqueeze(1)
+                                .to_broadcast([P, NJ, 64]),
                                 op=ALU.mult)
         n_i = const.tile([P, NJ, 64], I32, name="n_i")
         nc.vector.tensor_copy(out=n_i[:], in_=ang[:])
@@ -247,9 +247,9 @@ def tile_attention_pa_kernel(tc, x, w, out):
 
         t_x(0, "ss")
         q_x(0)
-        t_w(0, 0, "sssv", table_scalar)
+        t_w(0, 0, "sssv")
         q_w(0, 0)
-        t_w(0, 1, "sssv")
+        t_w(0, 1, "sssv", table_scalar)
         q_w(0, 1)
         t_x(1, "sv")
         q_x(1)

@@ -21,6 +21,7 @@ NJ = 4
 NG = 4
 NGRP = 4
 TWO_PI = 2.0 * math.pi
+HEAD_BANKS = 12
 
 
 def tile_attention_pa_kernel(tc, x, w, out):
@@ -125,6 +126,7 @@ def tile_attention_pa_kernel(tc, x, w, out):
         wc = {}
         ws = {}
         perm = {}
+        state = {"banks": 0}
 
         def permute(key, src, eng):
             t = ppool.tile([P, NG, 2, P], F32, name="wp")
@@ -137,7 +139,12 @@ def tile_attention_pa_kernel(tc, x, w, out):
 
         def t_tile(key, src, dst, engs):
             for gp in range(2):
-                bank = ps_t.tile([P, 2, 2, P], F32, name="tbank")
+                cnt = state["banks"]
+                state["banks"] = cnt + 1
+                if cnt < HEAD_BANKS and (cnt // 4) % 2 == 1:
+                    bank = ps_a.tile([P, 2, 2, P], F32, name="acc")
+                else:
+                    bank = ps_t.tile([P, 2, 2, P], F32, name="tbank")
                 for gg in range(2):
                     g = 2 * gp + gg
                     for u in range(2):
@@ -247,9 +254,9 @@ def tile_attention_pa_kernel(tc, x, w, out):
 
         t_x(0, "ss")
         q_x(0)
-        t_w(0, 0, "sssv")
+        t_w(0, 0, "svsv")
         q_w(0, 0)
-        t_w(0, 1, "sssv", table_scalar)
+        t_w(0, 1, "svsv", table_scalar)
         q_w(0, 1)
         t_x(1, "sv")
         q_x(1)

@@ -68,12 +68,14 @@ def tile_attention_pa_kernel(tc, x, w, out):
         ident = const.tile([P, P], F32, name="ident")
         make_identity(nc, ident[:])
 
-        dm = const.tile([P, 2], F32, name="dm")
-        nc.vector.memset(dm[:], 0.0)
-        nc.scalar.activation(out=dm[:, 1:2], in_=dm[:, 0:1], func=ACT.Sin)
+        sgn = const.tile([P, 2], F32, name="sgn")
+        nc.gpsimd.memset(sgn[:, 0:1], -1.0)
+        nc.gpsimd.memset(sgn[:, 1:2], 1.0)
 
         lh = const.tile([P, 2, 8], F32, name="lh")
         nc.vector.memset(lh[:, :, 0:1], 1.0)
+        dm = const.tile([P, 1], F32, name="dm")
+        nc.scalar.activation(out=dm[:], in_=lh[:, 0, 0:1], func=ACT.Sin)
         q = 10000.0 ** (-1.0 / 64.0)
         for s in range(3):
             wd = 1 << s
@@ -94,10 +96,8 @@ def tile_attention_pa_kernel(tc, x, w, out):
                                 op=ALU.mult)
         n_i = const.tile([P, NJ, 64], I32, name="n_i")
         nc.vector.tensor_copy(out=n_i[:], in_=ang[:])
-        n_f = const.tile([P, NJ, 64], F32, name="n_f")
-        nc.vector.tensor_copy(out=n_f[:], in_=n_i[:])
         fr = const.tile([P, NJ, 64], F32, name="fr")
-        nc.vector.tensor_tensor(out=fr[:], in0=ang[:], in1=n_f[:], op=ALU.subtract)
+        nc.vector.tensor_tensor(out=fr[:], in0=ang[:], in1=n_i[:], op=ALU.subtract)
         yn = const.tile([P, NJ, 64], F32, name="yn")
         nc.vector.scalar_tensor_tensor(out=yn[:], in0=fr[:], scalar=0.5, in1=fr[:],
                                        op0=ALU.is_gt, op1=ALU.subtract)
@@ -113,11 +113,14 @@ def tile_attention_pa_kernel(tc, x, w, out):
             nc.scalar.activation(out=sin_t[:], in_=yn[:], func=ACT.Sin, scale=-TWO_PI)
             nc.scalar.activation(out=cos_t[:], in_=ab[:], func=ACT.Sin, bias=math.pi / 2.0,
                                  scale=-TWO_PI)
-            for e in range(2):
-                nc.gpsimd.tensor_scalar(out=cos2[:, :, :, e], in0=cos_t[:], scalar1=1.0,
-                                        scalar2=0.0, op0=ALU.mult, op1=ALU.add)
-                nc.gpsimd.tensor_scalar(out=sin2[:, :, :, e], in0=sin_t[:], scalar1=2.0 * e - 1.0,
-                                        scalar2=0.0, op0=ALU.mult, op1=ALU.add)
+            nc.gpsimd.tensor_scalar(out=cos2[:], in0=cos_t[:].unsqueeze(3)
+                                    .to_broadcast([P, NJ, 64, 2]), scalar1=1.0,
+                                    scalar2=0.0, op0=ALU.mult, op1=ALU.add)
+            nc.gpsimd.tensor_tensor(out=sin2.rearrange("p j n e -> p (j n) e"),
+                                    in0=sin_t.rearrange("p j n -> p (j n)").unsqueeze(2)
+                                    .to_broadcast([P, NJ * 64, 2]),
+                                    in1=sgn[:].unsqueeze(1).to_broadcast([P, NJ * 64, 2]),
+                                    op=ALU.mult)
 
         xg = keep.tile([P, NJ, NG, P, 2], F32, name="xg", align_bytes=64)
         xc = keep.tile([P, NJ, NG, P], U32, name="xc", align_bytes=64)
@@ -228,7 +231,7 @@ def tile_attention_pa_kernel(tc, x, w, out):
                 nc.sync.dma_start(out=out_v[:, 4 * n:4 * n + 4, 2 * jp:2 * jp + 2, :], in_=r[:])
 
         runs = [[("x", 2), ("x", 3)]] + [[("w", m), ("w", m + 1)] for m in range(4, HEADS, 2)]
-        plan = {("x", 2): ("s", 1), ("w", 5): ("s", 1), ("w", 8): ("s", 2),
+        plan = {("x", 3): ("s", 1), ("w", 5): ("s", 1), ("w", 8): ("s", 2),
                 ("w", 10): ("s", 2), ("w", 12): ("s", 2),
                 ("w", 13): ("s", 1), ("w", 15): ("s", 1)}
 

from contextlib import ExitStack
import math

import concourse.mybir as mybir
from concourse.masks import make_identity

F32 = mybir.dt.float32
BF16 = mybir.dt.bfloat16
U32 = mybir.dt.uint32
U8 = mybir.dt.uint8
I32 = mybir.dt.int32
E5X4 = mybir.dt.float8_e5m2_x4
E4X4 = mybir.dt.float8_e4m3fn_x4
ALU = mybir.AluOpType
ACT = mybir.ActivationFunctionType

S_TOK, D_IN, HEADS, DH = 512, 2048, 16, 128
FLOPS = 2 * S_TOK * D_IN * HEADS * DH
P = 128
NJ = 4
NG = 4
NGRP = 4
TWO_PI = 2.0 * math.pi
HEAD_BANKS = 12


def tile_attention_pa_kernel(tc, x, w, out):
    nc = tc.nc
    with ExitStack() as ctx:
        const = ctx.enter_context(tc.tile_pool(name="const", bufs=1))
        raw = ctx.enter_context(tc.tile_pool(name="raw", bufs=1))
        keep = ctx.enter_context(tc.tile_pool(name="keep", bufs=1))
        wpool = ctx.enter_context(tc.tile_pool(name="wpool", bufs=2))
        ep = ctx.enter_context(tc.tile_pool(name="ep", bufs=3))
        ppool = ctx.enter_context(tc.tile_pool(name="ppool", bufs=4))
        ps_t = ctx.enter_context(tc.psum_pool(name="ps_t", bufs=4))
        ps_a = ctx.enter_context(tc.psum_pool(name="ps_a", bufs=4))
        ctx.enter_context(tc.manual_schedule())

        x_v = x.rearrange("(r j) k -> r j k", j=NJ)
        xr = []
        wr = []
        for j in range(NJ):
            xr.append(raw.tile([P, D_IN], BF16, name="xr%d" % j))
        for m in range(HEADS):
            wr.append(raw.tile([P, D_IN], BF16, name="wr%d" % m))

        def load_x(j, pieces):
            step = D_IN // pieces
            for c in range(pieces):
                nc.sync.dma_start(out=xr[j][:, step * c:step * (c + 1)],
                                  in_=x_v[:, j, step * c:step * (c + 1)])

        def load_w(m):
            nc.sync.dma_start(out=wr[m][:], in_=w[P * m:P * (m + 1), :])

        load_x(0, 2)
        for m in range(4):
            load_w(m)
        load_x(1, 1)
        load_x(2, 1)
        load_x(3, 1)
        for m in range(4, HEADS):
            load_w(m)

        idx_i = const.tile([P, NJ], I32, name="idx_i")
        nc.gpsimd.iota(idx_i[:], pattern=[[1, NJ]], base=0, channel_multiplier=NJ)
        ident = const.tile([P, P], F32, name="ident")
        make_identity(nc, ident[:])

        sgn = const.tile([P, 2], F32, name="sgn")
        nc.gpsimd.memset(sgn[:, 0:1], -1.0)
        nc.gpsimd.memset(sgn[:, 1:2], 1.0)

        lh = const.tile([P, 2, 8], F32, name="lh")
        nc.vector.memset(lh[:, :, 0:1], 1.0)
        dm = const.tile([P, 1], F32, name="dm")
        nc.scalar.activation(out=dm[:], in_=lh[:, 0, 0:1], func=ACT.Sin)
        q = 10000.0 ** (-1.0 / 64.0)
        for s in range(3):
            wd = 1 << s
            for c in range(2):
                nc.vector.tensor_scalar(out=lh[:, c, wd:2 * wd], in0=lh[:, c, 0:wd],
                                        scalar1=q ** (wd * (1 + 7 * c)), scalar2=None, op0=ALU.mult)
        idx_s = const.tile([P, NJ], F32, name="idx_s")
        nc.vector.tensor_scalar(out=idx_s[:], in0=idx_i[:], scalar1=1.0 / TWO_PI, scalar2=None,
                                op0=ALU.mult)
        th = const.tile([P, 8, 8], F32, name="th")
        nc.vector.tensor_tensor(out=th[:], in0=lh[:, 1, :].unsqueeze(2).to_broadcast([P, 8, 8]),
                                in1=lh[:, 0, :].unsqueeze(1).to_broadcast([P, 8, 8]),
                                op=ALU.mult)
        ang = const.tile([P, NJ, 64], F32, name="ang")
        nc.vector.tensor_tensor(out=ang[:], in0=idx_s[:].unsqueeze(2).to_broadcast([P, NJ, 64]),
                                in1=th.rearrange("p a b -> p (a b)").unsqueeze(1)
                                .to_broadcast([P, NJ, 64]),
                                op=ALU.mult)
        n_i = const.tile([P, NJ, 64], I32, name="n_i")
        nc.vector.tensor_copy(out=n_i[:], in_=ang[:])
        fr = const.tile([P, NJ, 64], F32, name="fr")
        nc.vector.tensor_tensor(out=fr[:], in0=ang[:], in1=n_i[:], op=ALU.subtract)
        yn = const.tile([P, NJ, 64], F32, name="yn")
        nc.vector.scalar_tensor_tensor(out=yn[:], in0=fr[:], scalar=0.5, in1=fr[:],
                                       op0=ALU.is_gt, op1=ALU.subtract)
        ab = const.tile([P, NJ, 64], F32, name="ab")
        nc.vector.scalar_tensor_tensor(out=ab[:], in0=yn[:], scalar=-1.0, in1=yn[:],
                                       op0=ALU.mult, op1=ALU.max)
        sin_t = const.tile([P, NJ, 64], F32, name="sin_t")
        cos_t = const.tile([P, NJ, 64], F32, name="cos_t")
        cos2 = const.tile([P, NJ, 64, 2], F32, name="cos2")
        sin2 = const.tile([P, NJ, 64, 2], F32, name="sin2")

        def table_scalar():
            nc.scalar.activation(out=sin_t[:], in_=yn[:], func=ACT.Sin, scale=-TWO_PI)
            nc.scalar.activation(out=cos_t[:], in_=ab[:], func=ACT.Sin, bias=math.pi / 2.0,
                                 scale=-TWO_PI)
            nc.gpsimd.tensor_scalar(out=cos2[:], in0=cos_t[:].unsqueeze(3)
                                    .to_broadcast([P, NJ, 64, 2]), scalar1=1.0,
                                    scalar2=0.0, op0=ALU.mult, op1=ALU.add)
            nc.gpsimd.tensor_tensor(out=sin2.rearrange("p j n e -> p (j n) e"),
                                    in0=sin_t.rearrange("p j n -> p (j n)").unsqueeze(2)
                                    .to_broadcast([P, NJ * 64, 2]),
                                    in1=sgn[:].unsqueeze(1).to_broadcast([P, NJ * 64, 2]),
                                    op=ALU.mult)

        xg = keep.tile([P, NJ, NG, P, 2], F32, name="xg", align_bytes=64)
        xc = keep.tile([P, NJ, NG, P], U32, name="xc", align_bytes=64)
        xs = keep.tile([P, NJ, NG, P], U8, name="xs", align_bytes=64)
        wg = {}
        wc = {}
        ws = {}
        perm = {}
        state = {"banks": 0}

        def permute(key, src, eng):
            t = ppool.tile([P, NG, 2, P], F32, name="wp")
            perm[key] = t
            view = src[:].bitcast(F32).rearrange("p (g q u) -> p g u q", g=NG, u=2)
            if eng == "s":
                nc.scalar.copy(out=t[:], in_=view)
            else:
                nc.vector.tensor_copy(out=t[:], in_=view)

        def t_tile(key, src, dst, engs):
            for gp in range(2):
                cnt = state["banks"]
                state["banks"] = cnt + 1
                if cnt < HEAD_BANKS and (cnt // 4) % 2 == 1:
                    bank = ps_a.tile([P, 2, 2, P], F32, name="acc")
                else:
                    bank = ps_t.tile([P, 2, 2, P], F32, name="tbank")
                for gg in range(2):
                    g = 2 * gp + gg
                    for u in range(2):
                        if key in perm:
                            in_ap = perm[key][:, g, u, :]
                        else:
                            in_ap = src[:].bitcast(F32)[:, 256 * g + u:256 * (g + 1):2]
                        nc.tensor.transpose(bank[:, gg, u, :], in_ap, ident[:])
                o = dst[:, 2 * gp:2 * gp + 2, :, :]
                i = bank.rearrange("p g u r -> p g r u")
                if engs[gp] == "s":
                    nc.scalar.copy(out=o, in_=i)
                else:
                    nc.vector.tensor_copy(out=o, in_=i)

        def t_x(j, engs):
            t_tile(("x", j), xr[j], xg[:, j], engs)

        def q_x(j):
            nc.vector.quantize_mx(
                out=xc[:, j].rearrange("p g r -> p (g r)").bitcast(E5X4),
                scales=xs[:, j].rearrange("p g r -> p (g r)"),
                in_=xg[:, j].rearrange("p g r u -> p (g r u)").bitcast(BF16))

        def t_w(n, hlf, engs, between=None):
            if hlf == 0:
                wg[n] = wpool.tile([P, NG, 512, 2], F32, name="wg", align_bytes=64)
                wc[n] = wpool.tile([P, NG, 512], U32, name="wc", align_bytes=64)
                ws[n] = wpool.tile([P, NG, 512], U8, name="ws", align_bytes=64)
            for c in range(2):
                m4 = 2 * hlf + c
                t_tile(("w", 4 * n + m4), wr[4 * n + m4],
                       wg[n][:, :, P * m4:P * (m4 + 1), :], engs[2 * c:2 * c + 2])
                if c == 0 and between is not None:
                    between()

        def q_w(n, hlf):
            cols = slice(256 * hlf, 256 * (hlf + 1))
            for g in range(NG):
                nc.vector.quantize_mx(
                    out=wc[n][:, g, cols].bitcast(E4X4),
                    scales=ws[n][:, g, cols],
                    in_=wg[n][:, g, cols, :].rearrange("p f u -> p (f u)").bitcast(BF16))

        acc = {}
        res = {}
        out_v = out.rearrange("h (r j) d -> r h j d", j=NJ)

        def mm(n, j):
            a = ps_a.tile([P, 512], F32, name="acc")
            acc[(n, j)] = a
            for g in range(NG):
                nc.tensor.matmul_mx(out=a[:], lhsT=xc[:, j, g, :].bitcast(E5X4),
                                    lhsT_scale=xs[:, j, g, :],
                                    rhs=wc[n][:, g, :].bitcast(E4X4),
                                    rhs_scale=ws[n][:, g, :],
                                    start=(g == 0), stop=(g == NG - 1))

        def rope(n, j, adder, split_store):
            jp = j // 2
            jj = j % 2
            if jj == 0:
                res[(n, jp)] = ep.tile([P, 4, 2, DH], F32, name="res")
            r = res[(n, jp)]
            a4 = acc[(n, j)].rearrange("p (h n e) -> p h n e", h=4, e=2)
            t1 = ep.tile([P, 4, 64, 2], F32, name="t1")
            t2 = ep.tile([P, 4, 64, 2], F32, name="t2")
            nc.vector.tensor_tensor(out=t1[:], in0=a4,
                                    in1=cos2[:, j].unsqueeze(1).to_broadcast([P, 4, 64, 2]),
                                    op=ALU.mult)
            nc.vector.tensor_tensor(out=t2[:], in0=a4[:, :, :, ::-1],
                                    in1=sin2[:, j].unsqueeze(1).to_broadcast([P, 4, 64, 2]),
                                    op=ALU.mult)
            add_eng = nc.gpsimd if adder == "g" else nc.vector
            add_eng.tensor_tensor(out=r[:, :, jj, :],
                                  in0=t1.rearrange("p h n e -> p h (n e)"),
                                  in1=t2.rearrange("p h n e -> p h (n e)"), op=ALU.add)
            if split_store:
                nc.sync.dma_start(out=out_v[:, 4 * n:4 * n + 4, j, :], in_=r[:, :, jj, :])
            elif jj == 1:
                nc.sync.dma_start(out=out_v[:, 4 * n:4 * n + 4, 2 * jp:2 * jp + 2, :], in_=r[:])

        runs = [[("x", 2), ("x", 3)]] + [[("w", m), ("w", m + 1)] for m in range(4, HEADS, 2)]
        plan = {("x", 3): ("s", 1), ("w", 5): ("s", 1), ("w", 8): ("s", 2),
                ("w", 10): ("s", 2), ("w", 12): ("s", 2),
                ("w", 13): ("s", 1), ("w", 15): ("s", 1)}

        def permutes_at(slot):
            for ri in range(len(runs)):
                for key in runs[ri]:
                    if key in plan and max(ri - plan[key][1], -1) == slot:
                        permute(key, xr[key[1]] if key[0] == "x" else wr[key[1]], plan[key][0])

        def do_run(ri):
            if ri == 0:
                t_x(2, "ss")
                t_x(3, "ss")
                permutes_at(0)
                q_x(2)
                q_x(3)
            else:
                n = 1 + (ri - 1) // 2
                hlf = (ri - 1) % 2
                t_w(n, hlf, "ssss")
                permutes_at(ri)
                q_w(n, hlf)

        t_x(0, "ss")
        q_x(0)
        t_w(0, 0, "svsv")
        q_w(0, 0)
        t_w(0, 1, "svsv", table_scalar)
        q_w(0, 1)
        t_x(1, "sv")
        q_x(1)
        permutes_at(-1)
        units = [1, 1, 1, 1, 2, 2, 2, 2, 2, 2]
        b = 0
        for ui in range(len(units)):
            banks = list(range(b, b + units[ui]))
            b += units[ui]
            for bb in banks:
                mm(bb // 4, bb % 4)
            for bb in banks:
                rope(bb // 4, bb % 4, "v" if bb == 15 else "g", bb >= 14)
            if ui < len(runs):
                do_run(ui)
